import numpy as np
import ml_dtypes


def mxq(x, axis, fmt="e4m3"):
    dtype, down = {"e4m3": (ml_dtypes.float8_e4m3fn, 7), "e5m2": (ml_dtypes.float8_e5m2, 14)}[fmt]
    v = np.moveaxis(np.asarray(x, np.float32).astype(ml_dtypes.bfloat16).astype(np.float64), axis, -1)
    blocks = v.reshape(v.shape[:-1] + (-1, 32))
    amax = np.abs(blocks).max(-1, keepdims=True)
    byte = np.maximum(np.where(amax > 0, np.frexp(amax)[1] - 1 + 127, 0) - down, 1)
    scale = np.exp2(byte - 127.0)
    codes = (blocks / scale).astype(np.float32).astype(dtype).astype(np.float64)
    return np.moveaxis((codes * scale).reshape(v.shape), -1, axis)


WIDE = False


def mx_kscale(k):
    if not WIDE:
        return np.ones(k)
    levels = np.array([10, -10, 5, -5, 0])
    a = np.random.permutation(np.resize(levels, k // 512 * 4)).reshape(k // 512, 4)
    idx = np.arange(k)
    return np.exp2(a[idx // 512, idx % 128 // 32])


BF16 = ml_dtypes.bfloat16


def bf(x):
    return np.asarray(x, np.float32).astype(BF16)


def f64(x):
    return np.asarray(x).astype(np.float64)


B, N_IN, N_H = 4096, 1024, 512
GLK, GB, GA, NOISE, DT = 0.1, 1.0, 0.8, 0.1, 0.1


def rho(v):
    return 1.0 / (1.0 + np.exp(-v))


def state():
    return np.random.standard_normal((B, N_H)) * 0.7 + np.random.standard_normal((B, 1)) * 0.7


def weight(n_out, n_in):
    return np.random.standard_normal((n_out, n_in)) * 4.0 / np.sqrt(n_in)


def setup_inputs():
    t = mx_kscale(N_IN)
    t = t / t.max()
    u = mx_kscale(N_H)
    u = u / u.max()
    return {"data": bf(np.random.standard_normal((B, N_IN)) + np.log(t)[None, :]), "s0": bf(state()),
            "s1": bf(state() + np.log(u)[None, :]), "i0": bf(state() + np.log(u)[None, :]),
            "wpf0": bf(weight(N_H, N_IN) / t[None, :]), "wpb0": bf(weight(N_H, N_H) / u[None, :]), "wpi0": bf(weight(N_H, N_H) / u[None, :]),
            "n_s0": bf(np.random.standard_normal((B, N_H)) * 2.0)}


def reference(data, s0, s1, i0, wpf0, wpb0, wpi0, n_s0):
    s0 = f64(s0)
    vb0 = mxq(rho(f64(data)), 1, "e4m3") @ mxq(f64(wpf0).T, 0, "e4m3")
    va_td0 = mxq(rho(f64(s1)), 1, "e4m3") @ mxq(f64(wpb0).T, 0, "e4m3")
    va_c0 = mxq(rho(f64(i0)), 1, "e4m3") @ mxq(f64(wpi0).T, 0, "e4m3")
    va0 = va_td0 + va_c0
    ds0 = -GLK * s0 + GB * (vb0 - s0) + GA * (va0 - s0) + NOISE * f64(n_s0)
    return s0 + DT * ds0

@@ -1,0 +1,252 @@
+from contextlib import ExitStack
+
+import concourse.mybir as mybir
+from concourse.masks import make_identity
+
+F32 = mybir.dt.float32
+BF16 = mybir.dt.bfloat16
+U32 = mybir.dt.uint32
+U8 = mybir.dt.uint8
+FP8X4 = mybir.dt.float8_e4m3fn_x4
+SIGMOID = mybir.ActivationFunctionType.Sigmoid
+MULT = mybir.AluOpType.mult
+ADD = mybir.AluOpType.add
+
+P = 128
+PACK = 4
+K_PASS = P * PACK
+WORDS = K_PASS // 2
+BANK = 512
+
+B, N_IN, N_H = 4096, 1024, 512
+TILES = B // P
+PASSES = (N_IN + N_H + N_H) // K_PASS
+BASAL_PASSES = (0, 1)
+APICAL_PASSES = (2, 3)
+
+GROUP = 4
+GROUPS = TILES // GROUP
+LEAD = 3
+
+DT, G_LEAK, G_BASAL, G_APICAL, NOISE_GAIN = 0.1, 0.1, 1.0, 0.8, 0.1
+KEEP = 1.0 - DT * (G_LEAK + G_BASAL + G_APICAL)
+BASAL = DT * G_BASAL
+APICAL = DT * G_APICAL
+NOISE = DT * NOISE_GAIN
+
+NOISE_LAG = 1
+QUANTISE_LAG = 2
+MULTIPLY_LAG = 3
+REST_LAG = 3
+BASAL_LAG = 4
+APICAL_LAG = 5
+
+FLOPS = 2 * B * (N_IN + N_H + N_H) * N_H
+
+
+def tile_dendriticnet_pa_t_kernel(tc, data, s0, s1, i0, wpf0, wpb0, wpi0, n_s0, out):
+    nc = tc.nc
+    by_tile = "(p t) c -> p t c"
+    data_v = data.rearrange(by_tile, t=TILES)
+    s0_v = s0.rearrange(by_tile, t=TILES)
+    s1_v = s1.rearrange(by_tile, t=TILES)
+    i0_v = i0.rearrange(by_tile, t=TILES)
+    noise_v = n_s0.rearrange(by_tile, t=TILES)
+    out_v = out.rearrange(by_tile, t=TILES)
+
+    with ExitStack() as ctx:
+        consts = ctx.enter_context(tc.tile_pool(name="consts", bufs=1))
+        inputs = ctx.enter_context(tc.tile_pool(name="inputs", bufs=LEAD + 2))
+        terms = ctx.enter_context(tc.tile_pool(name="terms", bufs=2))
+        somas = ctx.enter_context(tc.tile_pool(name="somas", bufs=3))
+        rates = ctx.enter_context(tc.tile_pool(name="rates", bufs=4))
+        quantised = ctx.enter_context(tc.tile_pool(name="quantised", bufs=3))
+        flipped = ctx.enter_context(tc.psum_pool(name="flipped", bufs=4))
+        sums = ctx.enter_context(tc.psum_pool(name="sums", bufs=4))
+        ctx.enter_context(tc.manual_schedule())
+
+        data_of, s1_of, i0_of, s0_of, noise_of = {}, {}, {}, {}, {}
+        soma_of = {}
+        term_of, rate_of, codes_of, scales_of, basal_of, apical_of = {}, {}, {}, {}, {}, {}
+
+        def load_inputs(g):
+            span = slice(g * GROUP, (g + 1) * GROUP)
+            data_sb = inputs.tile([P, GROUP, N_IN], BF16)
+            nc.sync.dma_start(out=data_sb[:], in_=data_v[:, span, :])
+            s1_sb = inputs.tile([P, GROUP, N_H], BF16)
+            nc.sync.dma_start(out=s1_sb[:], in_=s1_v[:, span, :])
+            i0_sb = inputs.tile([P, GROUP, N_H], BF16)
+            nc.sync.dma_start(out=i0_sb[:], in_=i0_v[:, span, :])
+            data_of[g], s1_of[g], i0_of[g] = data_sb, s1_sb, i0_sb
+
+        def load_state(g):
+            span = slice(g * GROUP, (g + 1) * GROUP)
+            noise_sb = inputs.tile([P, GROUP, N_H], BF16)
+            nc.sync.dma_start(out=noise_sb[:], in_=noise_v[:, span, :])
+            s0_sb = inputs.tile([P, GROUP, N_H], BF16)
+            nc.sync.dma_start(out=s0_sb[:], in_=s0_v[:, span, :])
+            noise_of[g], s0_of[g] = noise_sb, s0_sb
+
+        def pass_words(rows, first_word):
+            return rows.bitcast(F32)[:, first_word : first_word + WORDS]
+
+        def flip_pair(bank, first_words, second_words):
+            for local, words in enumerate((first_words, second_words)):
+                for u in range(2):
+                    column = u * 2 * P + local * P
+                    nc.tensor.transpose(
+                        out=bank[:, column : column + P],
+                        in_=words[:, u * P : (u + 1) * P],
+                        identity=ident[:],
+                    )
+
+        def rates_of_tile(t):
+            g, j = divmod(t, GROUP)
+            words = (
+                pass_words(data_of[g][:, j, :], 0),
+                pass_words(data_of[g][:, j, :], WORDS),
+                pass_words(s1_of[g][:, j, :], 0),
+                pass_words(i0_of[g][:, j, :], 0),
+            )
+            rate = rates.tile([P, PASSES * P * PACK], BF16, align_bytes=64)
+            for half in range(PASSES // 2):
+                bank = flipped.tile([P, BANK], F32)
+                flip_pair(bank, words[2 * half], words[2 * half + 1])
+                nc.scalar.activation(
+                    out=rate[:, half * 2 * BANK : (half + 1) * 2 * BANK].rearrange(
+                        "p (c u e) -> p c u e", u=2, e=2
+                    ),
+                    in_=bank[:].bitcast(BF16).rearrange("p (u c e) -> p c u e", u=2, e=2),
+                    func=SIGMOID,
+                )
+            rate_of[t] = rate
+
+        def quantise_tile(t):
+            codes = quantised.tile([P, PASSES * P], U32, align_bytes=64)
+            scales = quantised.tile([P, PASSES * P], U8, align_bytes=64)
+            nc.vector.quantize_mx(out=codes[:].bitcast(FP8X4), scales=scales[:], in_=rate_of[t][:])
+            codes_of[t], scales_of[t] = codes, scales
+
+        def multiply_tile(t, passes):
+            acc = sums.tile([P, N_H], F32)
+            for c in passes:
+                rows = slice(c * P, (c + 1) * P)
+                cols = slice(c * N_H, (c + 1) * N_H)
+                nc.tensor.matmul_mx(
+                    out=acc[:],
+                    lhsT=codes_of[t][:, rows].bitcast(FP8X4),
+                    lhsT_scale=scales_of[t][:, rows],
+                    rhs=w_codes[:, cols].bitcast(FP8X4),
+                    rhs_scale=w_scales[:, cols],
+                    start=(c == passes[0]),
+                    stop=(c == passes[-1]),
+                )
+            return acc
+
+        def noise_term(t):
+            g, j = divmod(t, GROUP)
+            term = terms.tile([P, N_H], F32)
+            nc.gpsimd.tensor_scalar(
+                out=term[:], in0=noise_of[g][:, j, :], scalar1=NOISE, scalar2=0.0, op0=MULT, op1=ADD
+            )
+            term_of[t] = term
+
+        def rest_term(t):
+            g, j = divmod(t, GROUP)
+            if j == 0:
+                soma = somas.tile([P, GROUP, N_H], F32)
+                soma_of[g] = soma
+            nc.vector.scalar_tensor_tensor(
+                out=soma_of[g][:, j, :], in0=s0_of[g][:, j, :], scalar=KEEP, in1=term_of[t][:], op0=MULT, op1=ADD
+            )
+
+        def add_product(t, acc, factor):
+            g, j = divmod(t, GROUP)
+            nc.vector.scalar_tensor_tensor(
+                out=soma_of[g][:, j, :], in0=acc[:], scalar=factor, in1=soma_of[g][:, j, :], op0=MULT, op1=ADD
+            )
+
+        def store_group(g):
+            nc.sync.dma_start(out=out_v[:, g * GROUP : (g + 1) * GROUP, :], in_=soma_of[g][:])
+
+        def prepare_weights():
+            sources = ((wpf_sb, 0), (wpf_sb, WORDS), (wpb_sb, 0), (wpi_sb, 0))
+            for c, (w_sb, first_word) in enumerate(sources):
+                for half in range(2):
+                    bank = sums.tile([P, BANK], F32, name="acc")
+                    flip_pair(
+                        bank,
+                        pass_words(w_sb[:, 2 * half, :], first_word),
+                        pass_words(w_sb[:, 2 * half + 1, :], first_word),
+                    )
+                    first = c * N_H * PACK + half * 2 * BANK
+                    nc.vector.tensor_copy(
+                        out=w_grouped[:, first : first + 2 * BANK].bitcast(F32).rearrange("p (c u) -> p c u", u=2),
+                        in_=bank[:].rearrange("p (u c) -> p c u", u=2),
+                    )
+                if c > 0:
+                    quantise_weights(c - 1)
+            quantise_weights(PASSES - 1)
+
+        def quantise_weights(c):
+            cols = slice(c * N_H, (c + 1) * N_H)
+            nc.vector.quantize_mx(
+                out=w_codes[:, cols].bitcast(FP8X4),
+                scales=w_scales[:, cols],
+                in_=w_grouped[:, c * N_H * PACK : (c + 1) * N_H * PACK],
+            )
+
+        def step(k):
+            def due(lag):
+                return 0 <= k - lag < TILES
+
+            if k % GROUP == 0 and k // GROUP + LEAD < GROUPS:
+                load_inputs(k // GROUP + LEAD)
+                load_state(k // GROUP + LEAD)
+            if due(0):
+                rates_of_tile(k)
+            if due(MULTIPLY_LAG):
+                basal_of[k - MULTIPLY_LAG] = multiply_tile(k - MULTIPLY_LAG, BASAL_PASSES)
+            if due(QUANTISE_LAG):
+                quantise_tile(k - QUANTISE_LAG)
+            if due(REST_LAG):
+                rest_term(k - REST_LAG)
+            if due(NOISE_LAG):
+                noise_term(k - NOISE_LAG)
+            if due(BASAL_LAG):
+                add_product(k - BASAL_LAG, basal_of[k - BASAL_LAG], BASAL)
+            if due(APICAL_LAG):
+                add_product(k - APICAL_LAG, apical_of[k - APICAL_LAG], APICAL)
+                if (k - APICAL_LAG) % GROUP == GROUP - 1:
+                    store_group((k - APICAL_LAG) // GROUP)
+            if due(MULTIPLY_LAG):
+                apical_of[k - MULTIPLY_LAG] = multiply_tile(k - MULTIPLY_LAG, APICAL_PASSES)
+
+        warm = consts.tile([P, 1], F32)
+        nc.vector.memset(warm[:], 0.0)
+        nc.scalar.activation(out=warm[:], in_=warm[:], func=SIGMOID)
+        ident = consts.tile([P, P], F32)
+        make_identity(nc, ident[:])
+
+        wpf_sb = consts.tile([P, N_H // P, N_IN], BF16)
+        wpb_sb = consts.tile([P, N_H // P, N_H], BF16)
+        wpi_sb = consts.tile([P, N_H // P, N_H], BF16)
+        w_grouped = consts.tile([P, PASSES * N_H * PACK], BF16, align_bytes=64)
+        w_codes = consts.tile([P, PASSES * N_H], U32, align_bytes=64)
+        w_scales = consts.tile([P, PASSES * N_H], U8, align_bytes=64)
+
+        load_inputs(0)
+        by_row_block = "(r p) k -> p r k"
+        nc.sync.dma_start(out=wpf_sb[:], in_=wpf0.rearrange(by_row_block, p=P))
+        nc.sync.dma_start(out=wpb_sb[:], in_=wpb0.rearrange(by_row_block, p=P))
+        nc.sync.dma_start(out=wpi_sb[:], in_=wpi0.rearrange(by_row_block, p=P))
+        load_state(0)
+        for g in range(1, LEAD):
+            load_inputs(g)
+            load_state(g)
+
+        for k in range(MULTIPLY_LAG):
+            step(k)
+        prepare_weights()
+        for k in range(MULTIPLY_LAG, TILES + APICAL_LAG):
+            step(k)

@@ -26,7 +26,7 @@ APICAL_PASSES = (2, 3)
 
 GROUP = 4
 GROUPS = TILES // GROUP
-LEAD = 3
+LEAD = 2
 
 DT, G_LEAK, G_BASAL, G_APICAL, NOISE_GAIN = 0.1, 0.1, 1.0, 0.8, 0.1
 KEEP = 1.0 - DT * (G_LEAK + G_BASAL + G_APICAL)
@@ -58,7 +58,7 @@ def tile_dendriticnet_pa_t_kernel(tc, data, s0, s1, i0, wpf0, wpb0, wpi0, n_s0, 
         consts = ctx.enter_context(tc.tile_pool(name="consts", bufs=1))
         inputs = ctx.enter_context(tc.tile_pool(name="inputs", bufs=LEAD + 2))
         terms = ctx.enter_context(tc.tile_pool(name="terms", bufs=2))
-        somas = ctx.enter_context(tc.tile_pool(name="somas", bufs=3))
+        somas = ctx.enter_context(tc.tile_pool(name="somas", bufs=4))
         rates = ctx.enter_context(tc.tile_pool(name="rates", bufs=4))
         quantised = ctx.enter_context(tc.tile_pool(name="quantised", bufs=3))
         flipped = ctx.enter_context(tc.psum_pool(name="flipped", bufs=4))
@@ -69,15 +69,17 @@ def tile_dendriticnet_pa_t_kernel(tc, data, s0, s1, i0, wpf0, wpb0, wpi0, n_s0, 
         soma_of = {}
         term_of, rate_of, codes_of, scales_of, basal_of, apical_of = {}, {}, {}, {}, {}, {}
 
-        def load_inputs(g):
-            span = slice(g * GROUP, (g + 1) * GROUP)
-            data_sb = inputs.tile([P, GROUP, N_IN], BF16)
-            nc.sync.dma_start(out=data_sb[:], in_=data_v[:, span, :])
-            s1_sb = inputs.tile([P, GROUP, N_H], BF16)
-            nc.sync.dma_start(out=s1_sb[:], in_=s1_v[:, span, :])
-            i0_sb = inputs.tile([P, GROUP, N_H], BF16)
-            nc.sync.dma_start(out=i0_sb[:], in_=i0_v[:, span, :])
-            data_of[g], s1_of[g], i0_of[g] = data_sb, s1_sb, i0_sb
+        def load_inputs(g, first=0, count=GROUP):
+            if first == 0:
+                data_sb = inputs.tile([P, GROUP, N_IN], BF16)
+                s1_sb = inputs.tile([P, GROUP, N_H], BF16)
+                i0_sb = inputs.tile([P, GROUP, N_H], BF16)
+                data_of[g], s1_of[g], i0_of[g] = data_sb, s1_sb, i0_sb
+            here = slice(first, first + count)
+            there = slice(g * GROUP + first, g * GROUP + first + count)
+            nc.sync.dma_start(out=data_of[g][:, here, :], in_=data_v[:, there, :])
+            nc.sync.dma_start(out=s1_of[g][:, here, :], in_=s1_v[:, there, :])
+            nc.sync.dma_start(out=i0_of[g][:, here, :], in_=i0_v[:, there, :])
 
         def load_state(g):
             span = slice(g * GROUP, (g + 1) * GROUP)
@@ -166,8 +168,12 @@ def tile_dendriticnet_pa_t_kernel(tc, data, s0, s1, i0, wpf0, wpb0, wpi0, n_s0, 
                 out=soma_of[g][:, j, :], in0=acc[:], scalar=factor, in1=soma_of[g][:, j, :], op0=MULT, op1=ADD
             )
 
-        def store_group(g):
-            nc.sync.dma_start(out=out_v[:, g * GROUP : (g + 1) * GROUP, :], in_=soma_of[g][:])
+        def store_finished(t):
+            g, j = divmod(t, GROUP)
+            if g == GROUPS - 1:
+                nc.sync.dma_start(out=out_v[:, t : t + 1, :], in_=soma_of[g][:, j : j + 1, :])
+            elif j == GROUP - 1:
+                nc.sync.dma_start(out=out_v[:, g * GROUP : (g + 1) * GROUP, :], in_=soma_of[g][:])
 
         def prepare_weights():
             sources = ((wpf_sb, 0), (wpf_sb, WORDS), (wpb_sb, 0), (wpi_sb, 0))
@@ -180,10 +186,12 @@ def tile_dendriticnet_pa_t_kernel(tc, data, s0, s1, i0, wpf0, wpb0, wpi0, n_s0, 
                         pass_words(w_sb[:, 2 * half + 1, :], first_word),
                     )
                     first = c * N_H * PACK + half * 2 * BANK
-                    nc.vector.tensor_copy(
-                        out=w_grouped[:, first : first + 2 * BANK].bitcast(F32).rearrange("p (c u) -> p c u", u=2),
-                        in_=bank[:].rearrange("p (u c) -> p c u", u=2),
-                    )
+                    grouped_words = w_grouped[:, first : first + 2 * BANK].bitcast(F32).rearrange("p (c u) -> p c u", u=2)
+                    flipped_words = bank[:].rearrange("p (u c) -> p c u", u=2)
+                    if half == 0:
+                        nc.vector.tensor_copy(out=grouped_words, in_=flipped_words)
+                    else:
+                        nc.scalar.copy(out=grouped_words, in_=flipped_words)
                 if c > 0:
                     quantise_weights(c - 1)
             quantise_weights(PASSES - 1)
@@ -217,8 +225,7 @@ def tile_dendriticnet_pa_t_kernel(tc, data, s0, s1, i0, wpf0, wpb0, wpi0, n_s0, 
                 add_product(k - BASAL_LAG, basal_of[k - BASAL_LAG], BASAL)
             if due(APICAL_LAG):
                 add_product(k - APICAL_LAG, apical_of[k - APICAL_LAG], APICAL)
-                if (k - APICAL_LAG) % GROUP == GROUP - 1:
-                    store_group((k - APICAL_LAG) // GROUP)
+                store_finished(k - APICAL_LAG)
             if due(MULTIPLY_LAG):
                 apical_of[k - MULTIPLY_LAG] = multiply_tile(k - MULTIPLY_LAG, APICAL_PASSES)
 
@@ -235,18 +242,17 @@ def tile_dendriticnet_pa_t_kernel(tc, data, s0, s1, i0, wpf0, wpb0, wpi0, n_s0, 
         w_codes = consts.tile([P, PASSES * N_H], U32, align_bytes=64)
         w_scales = consts.tile([P, PASSES * N_H], U8, align_bytes=64)
 
-        load_inputs(0)
         by_row_block = "(r p) k -> p r k"
         nc.sync.dma_start(out=wpf_sb[:], in_=wpf0.rearrange(by_row_block, p=P))
         nc.sync.dma_start(out=wpb_sb[:], in_=wpb0.rearrange(by_row_block, p=P))
         nc.sync.dma_start(out=wpi_sb[:], in_=wpi0.rearrange(by_row_block, p=P))
+        load_inputs(0, 0, GROUP // 2)
+        load_inputs(0, GROUP // 2, GROUP // 2)
         load_state(0)
         for g in range(1, LEAD):
             load_inputs(g)
             load_state(g)
 
-        for k in range(MULTIPLY_LAG):
-            step(k)
         prepare_weights()
-        for k in range(MULTIPLY_LAG, TILES + APICAL_LAG):
+        for k in range(TILES + APICAL_LAG):
             step(k)

@@ -34,10 +34,10 @@ BASAL = DT * G_BASAL
 APICAL = DT * G_APICAL
 NOISE = DT * NOISE_GAIN
 
-NOISE_LAG = 1
+NOISE_LAG = 0
 QUANTISE_LAG = 2
 MULTIPLY_LAG = 3
-REST_LAG = 3
+REST_LAG = 2
 BASAL_LAG = 4
 APICAL_LAG = 5
 
@@ -60,7 +60,7 @@ def tile_dendriticnet_pa_t_kernel(tc, data, s0, s1, i0, wpf0, wpb0, wpi0, n_s0, 
         terms = ctx.enter_context(tc.tile_pool(name="terms", bufs=2))
         somas = ctx.enter_context(tc.tile_pool(name="somas", bufs=4))
         rates = ctx.enter_context(tc.tile_pool(name="rates", bufs=4))
-        quantised = ctx.enter_context(tc.tile_pool(name="quantised", bufs=3))
+        quantised = ctx.enter_context(tc.tile_pool(name="quantised", bufs=4))
         flipped = ctx.enter_context(tc.psum_pool(name="flipped", bufs=4))
         sums = ctx.enter_context(tc.psum_pool(name="sums", bufs=4))
         ctx.enter_context(tc.manual_schedule())

@@ -35,11 +35,11 @@ APICAL = DT * G_APICAL
 NOISE = DT * NOISE_GAIN
 
 NOISE_LAG = 0
-QUANTISE_LAG = 2
-MULTIPLY_LAG = 3
 REST_LAG = 2
-BASAL_LAG = 4
-APICAL_LAG = 5
+QUANTISE_LAG = 2
+MULTIPLY_LAG = 2
+BASAL_LAG = 3
+APICAL_LAG = 4
 
 FLOPS = 2 * B * (N_IN + N_H + N_H) * N_H
 
@@ -81,13 +81,15 @@ def tile_dendriticnet_pa_t_kernel(tc, data, s0, s1, i0, wpf0, wpb0, wpi0, n_s0, 
             nc.sync.dma_start(out=s1_of[g][:, here, :], in_=s1_v[:, there, :])
             nc.sync.dma_start(out=i0_of[g][:, here, :], in_=i0_v[:, there, :])
 
-        def load_state(g):
-            span = slice(g * GROUP, (g + 1) * GROUP)
-            noise_sb = inputs.tile([P, GROUP, N_H], BF16)
-            nc.sync.dma_start(out=noise_sb[:], in_=noise_v[:, span, :])
-            s0_sb = inputs.tile([P, GROUP, N_H], BF16)
-            nc.sync.dma_start(out=s0_sb[:], in_=s0_v[:, span, :])
-            noise_of[g], s0_of[g] = noise_sb, s0_sb
+        def load_state(g, first=0, count=GROUP):
+            if first == 0:
+                noise_sb = inputs.tile([P, GROUP, N_H], BF16)
+                s0_sb = inputs.tile([P, GROUP, N_H], BF16)
+                noise_of[g], s0_of[g] = noise_sb, s0_sb
+            here = slice(first, first + count)
+            there = slice(g * GROUP + first, g * GROUP + first + count)
+            nc.sync.dma_start(out=noise_of[g][:, here, :], in_=noise_v[:, there, :])
+            nc.sync.dma_start(out=s0_of[g][:, here, :], in_=s0_v[:, there, :])
 
         def pass_words(rows, first_word):
             return rows.bitcast(F32)[:, first_word : first_word + WORDS]
@@ -213,14 +215,14 @@ def tile_dendriticnet_pa_t_kernel(tc, data, s0, s1, i0, wpf0, wpb0, wpi0, n_s0, 
                 load_state(k // GROUP + LEAD)
             if due(0):
                 rates_of_tile(k)
-            if due(MULTIPLY_LAG):
-                basal_of[k - MULTIPLY_LAG] = multiply_tile(k - MULTIPLY_LAG, BASAL_PASSES)
-            if due(QUANTISE_LAG):
-                quantise_tile(k - QUANTISE_LAG)
             if due(REST_LAG):
                 rest_term(k - REST_LAG)
             if due(NOISE_LAG):
                 noise_term(k - NOISE_LAG)
+            if due(QUANTISE_LAG):
+                quantise_tile(k - QUANTISE_LAG)
+            if due(MULTIPLY_LAG):
+                basal_of[k - MULTIPLY_LAG] = multiply_tile(k - MULTIPLY_LAG, BASAL_PASSES)
             if due(BASAL_LAG):
                 add_product(k - BASAL_LAG, basal_of[k - BASAL_LAG], BASAL)
             if due(APICAL_LAG):
@@ -246,12 +248,10 @@ def tile_dendriticnet_pa_t_kernel(tc, data, s0, s1, i0, wpf0, wpb0, wpi0, n_s0, 
         nc.sync.dma_start(out=wpf_sb[:], in_=wpf0.rearrange(by_row_block, p=P))
         nc.sync.dma_start(out=wpb_sb[:], in_=wpb0.rearrange(by_row_block, p=P))
         nc.sync.dma_start(out=wpi_sb[:], in_=wpi0.rearrange(by_row_block, p=P))
-        load_inputs(0, 0, GROUP // 2)
-        load_inputs(0, GROUP // 2, GROUP // 2)
-        load_state(0)
-        for g in range(1, LEAD):
-            load_inputs(g)
-            load_state(g)
+        for g in range(LEAD):
+            for first in (0, GROUP // 2):
+                load_inputs(g, first, GROUP // 2)
+                load_state(g, first, GROUP // 2)
 
         prepare_weights()
         for k in range(TILES + APICAL_LAG):

from contextlib import ExitStack

import concourse.mybir as mybir
from concourse.masks import make_identity

F32 = mybir.dt.float32
BF16 = mybir.dt.bfloat16
U32 = mybir.dt.uint32
U8 = mybir.dt.uint8
FP8X4 = mybir.dt.float8_e4m3fn_x4
SIGMOID = mybir.ActivationFunctionType.Sigmoid
MULT = mybir.AluOpType.mult
ADD = mybir.AluOpType.add

P = 128
PACK = 4
K_PASS = P * PACK
WORDS = K_PASS // 2
BANK = 512

B, N_IN, N_H = 4096, 1024, 512
TILES = B // P
PASSES = (N_IN + N_H + N_H) // K_PASS
BASAL_PASSES = (0, 1)
APICAL_PASSES = (2, 3)

GROUP = 4
GROUPS = TILES // GROUP
LEAD = 2

DT, G_LEAK, G_BASAL, G_APICAL, NOISE_GAIN = 0.1, 0.1, 1.0, 0.8, 0.1
KEEP = 1.0 - DT * (G_LEAK + G_BASAL + G_APICAL)
BASAL = DT * G_BASAL
APICAL = DT * G_APICAL
NOISE = DT * NOISE_GAIN

NOISE_LAG = 0
REST_LAG = 2
QUANTISE_LAG = 2
MULTIPLY_LAG = 2
BASAL_LAG = 3
APICAL_LAG = 4

FLOPS = 2 * B * (N_IN + N_H + N_H) * N_H


def tile_dendriticnet_pa_t_kernel(tc, data, s0, s1, i0, wpf0, wpb0, wpi0, n_s0, out):
    nc = tc.nc
    by_tile = "(p t) c -> p t c"
    data_v = data.rearrange(by_tile, t=TILES)
    s0_v = s0.rearrange(by_tile, t=TILES)
    s1_v = s1.rearrange(by_tile, t=TILES)
    i0_v = i0.rearrange(by_tile, t=TILES)
    noise_v = n_s0.rearrange(by_tile, t=TILES)
    out_v = out.rearrange(by_tile, t=TILES)

    with ExitStack() as ctx:
        consts = ctx.enter_context(tc.tile_pool(name="consts", bufs=1))
        inputs = ctx.enter_context(tc.tile_pool(name="inputs", bufs=LEAD + 2))
        terms = ctx.enter_context(tc.tile_pool(name="terms", bufs=2))
        somas = ctx.enter_context(tc.tile_pool(name="somas", bufs=4))
        rates = ctx.enter_context(tc.tile_pool(name="rates", bufs=4))
        quantised = ctx.enter_context(tc.tile_pool(name="quantised", bufs=4))
        flipped = ctx.enter_context(tc.psum_pool(name="flipped", bufs=4))
        sums = ctx.enter_context(tc.psum_pool(name="sums", bufs=4))
        ctx.enter_context(tc.manual_schedule())

        data_of, s1_of, i0_of, s0_of, noise_of = {}, {}, {}, {}, {}
        soma_of = {}
        term_of, rate_of, codes_of, scales_of, basal_of, apical_of = {}, {}, {}, {}, {}, {}

        def load_inputs(g, first=0, count=GROUP):
            if first == 0:
                data_sb = inputs.tile([P, GROUP, N_IN], BF16)
                s1_sb = inputs.tile([P, GROUP, N_H], BF16)
                i0_sb = inputs.tile([P, GROUP, N_H], BF16)
                data_of[g], s1_of[g], i0_of[g] = data_sb, s1_sb, i0_sb
            here = slice(first, first + count)
            there = slice(g * GROUP + first, g * GROUP + first + count)
            nc.sync.dma_start(out=data_of[g][:, here, :], in_=data_v[:, there, :])
            nc.sync.dma_start(out=s1_of[g][:, here, :], in_=s1_v[:, there, :])
            nc.sync.dma_start(out=i0_of[g][:, here, :], in_=i0_v[:, there, :])

        def load_state(g, first=0, count=GROUP):
            if first == 0:
                noise_sb = inputs.tile([P, GROUP, N_H], BF16)
                s0_sb = inputs.tile([P, GROUP, N_H], BF16)
                noise_of[g], s0_of[g] = noise_sb, s0_sb
            here = slice(first, first + count)
            there = slice(g * GROUP + first, g * GROUP + first + count)
            nc.sync.dma_start(out=noise_of[g][:, here, :], in_=noise_v[:, there, :])
            nc.sync.dma_start(out=s0_of[g][:, here, :], in_=s0_v[:, there, :])

        def pass_words(rows, first_word):
            return rows.bitcast(F32)[:, first_word : first_word + WORDS]

        def flip_pair(bank, first_words, second_words):
            for local, words in enumerate((first_words, second_words)):
                for u in range(2):
                    column = u * 2 * P + local * P
                    nc.tensor.transpose(
                        out=bank[:, column : column + P],
                        in_=words[:, u * P : (u + 1) * P],
                        identity=ident[:],
                    )

        def rates_of_tile(t):
            g, j = divmod(t, GROUP)
            words = (
                pass_words(data_of[g][:, j, :], 0),
                pass_words(data_of[g][:, j, :], WORDS),
                pass_words(s1_of[g][:, j, :], 0),
                pass_words(i0_of[g][:, j, :], 0),
            )
            rate = rates.tile([P, PASSES * P * PACK], BF16, align_bytes=64)
            for half in range(PASSES // 2):
                bank = flipped.tile([P, BANK], F32)
                flip_pair(bank, words[2 * half], words[2 * half + 1])
                nc.scalar.activation(
                    out=rate[:, half * 2 * BANK : (half + 1) * 2 * BANK].rearrange(
                        "p (c u e) -> p c u e", u=2, e=2
                    ),
                    in_=bank[:].bitcast(BF16).rearrange("p (u c e) -> p c u e", u=2, e=2),
                    func=SIGMOID,
                )
            rate_of[t] = rate

        def quantise_tile(t):
            codes = quantised.tile([P, PASSES * P], U32, align_bytes=64)
            scales = quantised.tile([P, PASSES * P], U8, align_bytes=64)
            nc.vector.quantize_mx(out=codes[:].bitcast(FP8X4), scales=scales[:], in_=rate_of[t][:])
            codes_of[t], scales_of[t] = codes, scales

        def multiply_tile(t, passes):
            acc = sums.tile([P, N_H], F32)
            for c in passes:
                rows = slice(c * P, (c + 1) * P)
                cols = slice(c * N_H, (c + 1) * N_H)
                nc.tensor.matmul_mx(
                    out=acc[:],
                    lhsT=codes_of[t][:, rows].bitcast(FP8X4),
                    lhsT_scale=scales_of[t][:, rows],
                    rhs=w_codes[:, cols].bitcast(FP8X4),
                    rhs_scale=w_scales[:, cols],
                    start=(c == passes[0]),
                    stop=(c == passes[-1]),
                )
            return acc

        def noise_term(t):
            g, j = divmod(t, GROUP)
            term = terms.tile([P, N_H], F32)
            nc.gpsimd.tensor_scalar(
                out=term[:], in0=noise_of[g][:, j, :], scalar1=NOISE, scalar2=0.0, op0=MULT, op1=ADD
            )
            term_of[t] = term

        def rest_term(t):
            g, j = divmod(t, GROUP)
            if j == 0:
                soma = somas.tile([P, GROUP, N_H], F32)
                soma_of[g] = soma
            nc.vector.scalar_tensor_tensor(
                out=soma_of[g][:, j, :], in0=s0_of[g][:, j, :], scalar=KEEP, in1=term_of[t][:], op0=MULT, op1=ADD
            )

        def add_product(t, acc, factor):
            g, j = divmod(t, GROUP)
            nc.vector.scalar_tensor_tensor(
                out=soma_of[g][:, j, :], in0=acc[:], scalar=factor, in1=soma_of[g][:, j, :], op0=MULT, op1=ADD
            )

        def store_finished(t):
            g, j = divmod(t, GROUP)
            if g == GROUPS - 1:
                nc.sync.dma_start(out=out_v[:, t : t + 1, :], in_=soma_of[g][:, j : j + 1, :])
            elif j == GROUP - 1:
                nc.sync.dma_start(out=out_v[:, g * GROUP : (g + 1) * GROUP, :], in_=soma_of[g][:])

        def prepare_weights():
            sources = ((wpf_sb, 0), (wpf_sb, WORDS), (wpb_sb, 0), (wpi_sb, 0))
            for c, (w_sb, first_word) in enumerate(sources):
                for half in range(2):
                    bank = sums.tile([P, BANK], F32, name="acc")
                    flip_pair(
                        bank,
                        pass_words(w_sb[:, 2 * half, :], first_word),
                        pass_words(w_sb[:, 2 * half + 1, :], first_word),
                    )
                    first = c * N_H * PACK + half * 2 * BANK
                    grouped_words = w_grouped[:, first : first + 2 * BANK].bitcast(F32).rearrange("p (c u) -> p c u", u=2)
                    flipped_words = bank[:].rearrange("p (u c) -> p c u", u=2)
                    if half == 0:
                        nc.vector.tensor_copy(out=grouped_words, in_=flipped_words)
                    else:
                        nc.scalar.copy(out=grouped_words, in_=flipped_words)
                if c > 0:
                    quantise_weights(c - 1)
            quantise_weights(PASSES - 1)

        def quantise_weights(c):
            cols = slice(c * N_H, (c + 1) * N_H)
            nc.vector.quantize_mx(
                out=w_codes[:, cols].bitcast(FP8X4),
                scales=w_scales[:, cols],
                in_=w_grouped[:, c * N_H * PACK : (c + 1) * N_H * PACK],
            )

        def step(k):
            def due(lag):
                return 0 <= k - lag < TILES

            if k % GROUP == 0 and k // GROUP + LEAD < GROUPS:
                load_inputs(k // GROUP + LEAD)
                load_state(k // GROUP + LEAD)
            if due(0):
                rates_of_tile(k)
            if due(REST_LAG):
                rest_term(k - REST_LAG)
            if due(NOISE_LAG):
                noise_term(k - NOISE_LAG)
            if due(QUANTISE_LAG):
                quantise_tile(k - QUANTISE_LAG)
            if due(MULTIPLY_LAG):
                basal_of[k - MULTIPLY_LAG] = multiply_tile(k - MULTIPLY_LAG, BASAL_PASSES)
            if due(BASAL_LAG):
                add_product(k - BASAL_LAG, basal_of[k - BASAL_LAG], BASAL)
            if due(APICAL_LAG):
                add_product(k - APICAL_LAG, apical_of[k - APICAL_LAG], APICAL)
                store_finished(k - APICAL_LAG)
            if due(MULTIPLY_LAG):
                apical_of[k - MULTIPLY_LAG] = multiply_tile(k - MULTIPLY_LAG, APICAL_PASSES)

        warm = consts.tile([P, 1], F32)
        nc.vector.memset(warm[:], 0.0)
        nc.scalar.activation(out=warm[:], in_=warm[:], func=SIGMOID)
        ident = consts.tile([P, P], F32)
        make_identity(nc, ident[:])

        wpf_sb = consts.tile([P, N_H // P, N_IN], BF16)
        wpb_sb = consts.tile([P, N_H // P, N_H], BF16)
        wpi_sb = consts.tile([P, N_H // P, N_H], BF16)
        w_grouped = consts.tile([P, PASSES * N_H * PACK], BF16, align_bytes=64)
        w_codes = consts.tile([P, PASSES * N_H], U32, align_bytes=64)
        w_scales = consts.tile([P, PASSES * N_H], U8, align_bytes=64)

        by_row_block = "(r p) k -> p r k"
        nc.sync.dma_start(out=wpf_sb[:], in_=wpf0.rearrange(by_row_block, p=P))
        nc.sync.dma_start(out=wpb_sb[:], in_=wpb0.rearrange(by_row_block, p=P))
        nc.sync.dma_start(out=wpi_sb[:], in_=wpi0.rearrange(by_row_block, p=P))
        for g in range(LEAD):
            for first in (0, GROUP // 2):
                load_inputs(g, first, GROUP // 2)
                load_state(g, first, GROUP // 2)

        prepare_weights()
        for k in range(TILES + APICAL_LAG):
            step(k)
